import numpy as np
import ml_dtypes

BF16 = ml_dtypes.bfloat16


def bf(x):
    return np.asarray(x, np.float32).astype(BF16)


def f32(x):
    return np.asarray(x, np.float32)


def f64(x):
    return np.asarray(x).astype(np.float64)


def striped(idx):
    return np.tile(idx.reshape(-1, 16).T, (8, 1))


S, D, M, N, K = 4096, 128, 128, 4096, 8


def setup_inputs():
    return {"table": bf(np.random.standard_normal((S, D))),
            "w1": bf(np.random.standard_normal((D, M)) / np.sqrt(D)),
            "b1": f32(0.1 * np.random.standard_normal((M, 1))),
            "w2": bf(np.random.standard_normal((M, M)) / np.sqrt(M)),
            "b2": f32(0.1 * np.random.standard_normal((M, 1))),
            "w3": bf(np.random.standard_normal((M, M)) / np.sqrt(M)),
            "b3": f32(0.1 * np.random.standard_normal((M, 1))),
            "offs": striped(np.random.permutation(S)[:N])}


def reference(table, w1, b1, w2, b2, w3, b3, offs):
    idx = offs[:16].T.reshape(-1)
    h = np.maximum(f64(w1).T @ f64(table)[idx].T + f64(b1), 0.0)
    h = np.maximum(f64(w2).T @ h + f64(b2), 0.0)
    h = np.maximum(f64(w3).T @ h + f64(b3), 0.0)
    return h.reshape(M, N // K, K).max(axis=-1)

@@ -1,0 +1,118 @@
+import concourse.mybir as mybir
+from concourse.masks import make_identity
+
+BF16, F32, U16 = mybir.dt.bfloat16, mybir.dt.float32, mybir.dt.uint16
+ADD, MAX = mybir.AluOpType.add, mybir.AluOpType.max
+RELU = mybir.ActivationFunctionType.Relu
+
+P = 128
+POINTS = 4096
+ENTRIES = 4096
+BALL = 8
+PIECE = 512
+N_PIECES = ENTRIES // PIECE
+GROUP = 4
+N_GROUPS = POINTS // (GROUP * P)
+UNITS = (2,) + (1,) * (N_GROUPS - 2) + (2,)
+WARM_UP = 3
+CHUNKS = (PIECE // 2,) * (2 * N_PIECES)
+LAG = 3
+LAST = 2
+
+FLOPS = 2 * ENTRIES * P * P * 3
+
+
+def tile_setabstraction_kernel(tc, table, w1, b1, w2, b2, w3, b3, offs, out):
+    nc = tc.nc
+    with (
+        tc.tile_pool(name="held", bufs=1) as held,
+        tc.psum_pool(name="psum", bufs=8) as psum,
+    ):
+        zeros = held.tile([P, PIECE], BF16, name="zeros")
+        nc.vector.memset(zeros[:], 0.0)
+
+        def idle_matmul():
+            unread = psum.tile([P, PIECE], F32, name="unread", tag="bank")
+            nc.tensor.matmul(unread[:], zeros[:, :P], zeros[:], start=True, stop=True)
+
+        for n in range(WARM_UP):
+            idle_matmul()
+
+        identity = held.tile([P, P], BF16, name="identity")
+        make_identity(nc, identity[:])
+
+        rows = held.tile([P, N_GROUPS, GROUP, P], BF16, name="rows")
+        for g in range(N_GROUPS):
+            group_points = table[g * GROUP * P : (g + 1) * GROUP * P, :]
+            nc.sync.dma_start(
+                rows[:, g, :, :].rearrange("p (u j) d -> p u j d", u=UNITS[g]),
+                group_points.rearrange("(u p j) d -> p u j d", u=UNITS[g], p=P),
+            )
+        offsets = held.tile([P, ENTRIES // 16], U16, name="offsets")
+        nc.sync.dma_start(offsets[:], offs)
+        weights = [held.tile([P, P], BF16, name=f"w{layer}") for layer in range(3)]
+        biases = [held.tile([P, 1], F32, name=f"b{layer}") for layer in range(3)]
+        nc.gpsimd.dma_start(weights[0][:], w1)
+        nc.gpsimd.dma_start(biases[0][:], b1)
+        for layer, (w, b) in enumerate(((w2, b2), (w3, b3)), start=1):
+            nc.sync.dma_start(weights[layer][:], w)
+            nc.sync.dma_start(biases[layer][:], b)
+
+        scratch = held.tile([P, 1], F32, name="scratch")
+        nc.vector.memset(scratch[:], 0.0)
+        nc.scalar.activation(scratch[:], scratch[:], RELU)
+
+        window = held.tile([P, POINTS], BF16, name="window")
+        n_units = 0
+        for g in range(N_GROUPS):
+            blocks = GROUP // UNITS[g]
+            for u in range(UNITS[g]):
+                flipped = psum.tile([P, blocks, P], BF16, name="flipped", tag="bank")
+                for j in range(blocks):
+                    nc.tensor.transpose(flipped[:, j, :], rows[:, g, u * blocks + j, :], identity[:])
+                first = (g * GROUP + u * blocks) * P
+                columns = window[:, first : first + blocks * P].rearrange("d (p j) -> d p j", j=blocks)
+                in_point_order = flipped[:].rearrange("d j p -> d p j")
+                if n_units % 2 == 0:
+                    nc.vector.tensor_copy(columns, in_point_order)
+                else:
+                    nc.scalar.copy(columns, in_point_order)
+                n_units += 1
+            if g % 2 == 1:
+                idle_matmul()
+
+        h1 = held.tile([P, ENTRIES], BF16, name="h1")
+        for i in range(N_PIECES):
+            sum1 = psum.tile([P, PIECE], F32, name="sum1", tag="bank")
+            looked_up = window[:].indirect(offsets[:, i * (PIECE // 16) : (i + 1) * (PIECE // 16)])
+            nc.tensor.matmul(sum1[:], weights[0][:], looked_up, start=True, stop=True)
+            piece = slice(i * PIECE, (i + 1) * PIECE)
+            if i % 2 == 0:
+                nc.scalar.activation(h1[:, piece], sum1[:], RELU, bias=biases[0][:])
+            else:
+                nc.vector.tensor_scalar(h1[:, piece], sum1[:], biases[0][:], 0.0, ADD, MAX)
+
+        h2 = held.tile([P, ENTRIES], BF16, name="h2")
+        pooled = held.tile([P, ENTRIES // BALL], F32, name="pooled")
+        chunk_entries = [slice(sum(CHUNKS[:c]), sum(CHUNKS[: c + 1])) for c in range(len(CHUNKS))]
+        for step in range(len(CHUNKS) + LAG):
+            if step < len(CHUNKS):
+                entries, width = chunk_entries[step], CHUNKS[step]
+                sum2 = psum.tile([P, PIECE], F32, name="sum2", tag="bank")
+                nc.tensor.matmul(sum2[:, :width], weights[1][:], h1[:, entries], start=True, stop=True)
+                nc.scalar.activation(h2[:, entries], sum2[:, :width], RELU, bias=biases[1][:])
+            if step >= LAG:
+                entries, width = chunk_entries[step - LAG], CHUNKS[step - LAG]
+                sum3 = psum.tile([P, PIECE], F32, name="sum3", tag="bank")
+                nc.tensor.matmul(sum3[:, :width], weights[2][:], h2[:, entries], start=True, stop=True)
+                balls = slice(entries.start // BALL, entries.stop // BALL)
+                nc.vector.tensor_reduce(
+                    pooled[:, balls], sum3[:, :width].rearrange("r (q k) -> r q k", k=BALL), mybir.AxisListType.X, MAX
+                )
+
+        result = held.tile([P, ENTRIES // BALL], F32, name="result")
+        early = (N_PIECES - LAST) * (PIECE // BALL)
+        nc.scalar.activation(result[:, :early], pooled[:, :early], RELU, bias=biases[2][:])
+        nc.scalar.dma_start(out[:, :early], result[:, :early])
+        nc.vector.tensor_scalar(result[:, early:], pooled[:, early:], biases[2][:], 0.0, ADD, MAX)
+        nc.sync.dma_start(out[:, early:], result[:, early:])

@@ -14,6 +14,7 @@ N_PIECES = ENTRIES // PIECE
 GROUP = 4
 N_GROUPS = POINTS // (GROUP * P)
 UNITS = (2,) + (1,) * (N_GROUPS - 2) + (2,)
+BLOCKWISE = range(N_GROUPS - 2, N_GROUPS)
 WARM_UP = 3
 CHUNKS = (PIECE // 2,) * (2 * N_PIECES)
 LAG = 3
@@ -46,7 +47,9 @@ def tile_setabstraction_kernel(tc, table, w1, b1, w2, b2, w3, b3, offs, out):
             group_points = table[g * GROUP * P : (g + 1) * GROUP * P, :]
             nc.sync.dma_start(
                 rows[:, g, :, :].rearrange("p (u j) d -> p u j d", u=UNITS[g]),
-                group_points.rearrange("(u p j) d -> p u j d", u=UNITS[g], p=P),
+                group_points.rearrange(
+                    "(u j p) d -> p u j d" if g in BLOCKWISE else "(u p j) d -> p u j d", u=UNITS[g], p=P
+                ),
             )
         offsets = held.tile([P, ENTRIES // 16], U16, name="offsets")
         nc.sync.dma_start(offsets[:], offs)
@@ -71,8 +74,13 @@ def tile_setabstraction_kernel(tc, table, w1, b1, w2, b2, w3, b3, offs, out):
                 for j in range(blocks):
                     nc.tensor.transpose(flipped[:, j, :], rows[:, g, u * blocks + j, :], identity[:])
                 first = (g * GROUP + u * blocks) * P
-                columns = window[:, first : first + blocks * P].rearrange("d (p j) -> d p j", j=blocks)
-                in_point_order = flipped[:].rearrange("d j p -> d p j")
+                columns = window[:, first : first + blocks * P]
+                if g in BLOCKWISE:
+                    columns = columns.rearrange("d (j p) -> d j p", j=blocks)
+                    in_point_order = flipped[:]
+                else:
+                    columns = columns.rearrange("d (p j) -> d p j", j=blocks)
+                    in_point_order = flipped[:].rearrange("d j p -> d p j")
                 if n_units % 2 == 0:
                     nc.vector.tensor_copy(columns, in_point_order)
                 else:

@@ -16,9 +16,13 @@ N_GROUPS = POINTS // (GROUP * P)
 UNITS = (2,) + (1,) * (N_GROUPS - 2) + (2,)
 BLOCKWISE = range(N_GROUPS - 2, N_GROUPS)
 WARM_UP = 3
-CHUNKS = (PIECE // 2,) * (2 * N_PIECES)
-LAG = 3
-LAST = 2
+CHUNKS = (PIECE // 2,) * (2 * N_PIECES - 1) + (PIECE // 4,) * 2
+FIRST_RUN = 5
+SECOND_EARLY = 2 * FIRST_RUN
+THIRD_EARLY = 8
+N_HALVED = 24 - SECOND_EARLY - THIRD_EARLY
+MIDDLE_LAG, LAST_LAG = 6, 3
+VECTOR_H2 = (*range(0, MIDDLE_LAG, 2), SECOND_EARLY)
 
 FLOPS = 2 * ENTRIES * P * P * 3
 
@@ -90,37 +94,73 @@ def tile_setabstraction_kernel(tc, table, w1, b1, w2, b2, w3, b3, offs, out):
                 idle_matmul()
 
         h1 = held.tile([P, ENTRIES], BF16, name="h1")
-        for i in range(N_PIECES):
-            sum1 = psum.tile([P, PIECE], F32, name="sum1", tag="bank")
-            looked_up = window[:].indirect(offsets[:, i * (PIECE // 16) : (i + 1) * (PIECE // 16)])
-            nc.tensor.matmul(sum1[:], weights[0][:], looked_up, start=True, stop=True)
-            piece = slice(i * PIECE, (i + 1) * PIECE)
-            if i % 2 == 0:
-                nc.scalar.activation(h1[:, piece], sum1[:], RELU, bias=biases[0][:])
-            else:
-                nc.vector.tensor_scalar(h1[:, piece], sum1[:], biases[0][:], 0.0, ADD, MAX)
-
         h2 = held.tile([P, ENTRIES], BF16, name="h2")
         pooled = held.tile([P, ENTRIES // BALL], F32, name="pooled")
+
+        def first_layer(pieces):
+            for i in pieces:
+                sum1 = psum.tile([P, PIECE], F32, name="sum1", tag="bank")
+                looked_up = window[:].indirect(offsets[:, i * (PIECE // 16) : (i + 1) * (PIECE // 16)])
+                nc.tensor.matmul(sum1[:], weights[0][:], looked_up, start=True, stop=True)
+                piece = slice(i * PIECE, (i + 1) * PIECE)
+                if (i - pieces[0]) % 2 == 0:
+                    nc.scalar.activation(h1[:, piece], sum1[:], RELU, bias=biases[0][:])
+                else:
+                    nc.vector.tensor_scalar(h1[:, piece], sum1[:], biases[0][:], 0.0, ADD, MAX)
+
         chunk_entries = [slice(sum(CHUNKS[:c]), sum(CHUNKS[: c + 1])) for c in range(len(CHUNKS))]
-        for step in range(len(CHUNKS) + LAG):
-            if step < len(CHUNKS):
-                entries, width = chunk_entries[step], CHUNKS[step]
-                sum2 = psum.tile([P, PIECE], F32, name="sum2", tag="bank")
-                nc.tensor.matmul(sum2[:, :width], weights[1][:], h1[:, entries], start=True, stop=True)
-                nc.scalar.activation(h2[:, entries], sum2[:, :width], RELU, bias=biases[1][:])
-            if step >= LAG:
-                entries, width = chunk_entries[step - LAG], CHUNKS[step - LAG]
-                sum3 = psum.tile([P, PIECE], F32, name="sum3", tag="bank")
-                nc.tensor.matmul(sum3[:, :width], weights[2][:], h2[:, entries], start=True, stop=True)
-                balls = slice(entries.start // BALL, entries.stop // BALL)
-                nc.vector.tensor_reduce(
-                    pooled[:, balls], sum3[:, :width].rearrange("r (q k) -> r q k", k=BALL), mybir.AxisListType.X, MAX
+
+        def plain_product(layer, source, c, parts):
+            total = psum.tile([P, CHUNKS[c]], F32, name="total", tag="bank")
+            width = CHUNKS[c] // parts
+            for n in range(parts):
+                first = chunk_entries[c].start + n * width
+                nc.tensor.matmul(
+                    total[:, n * width : (n + 1) * width],
+                    weights[layer][:],
+                    source[:, first : first + width],
+                    start=True,
+                    stop=True,
                 )
+            return total
+
+        def second_layer(c):
+            sum2 = plain_product(1, h1, c, 1)
+            if c in VECTOR_H2:
+                nc.vector.tensor_scalar(h2[:, chunk_entries[c]], sum2[:], biases[1][:], 0.0, ADD, MAX)
+            else:
+                nc.scalar.activation(h2[:, chunk_entries[c]], sum2[:], RELU, bias=biases[1][:])
+
+        def third_layer(c):
+            sum3 = plain_product(2, h2, c, 2 if c < N_HALVED else 1)
+            balls = slice(chunk_entries[c].start // BALL, chunk_entries[c].stop // BALL)
+            nc.vector.tensor_reduce(
+                pooled[:, balls], sum3[:].rearrange("r (q k) -> r q k", k=BALL), mybir.AxisListType.X, MAX
+            )
 
         result = held.tile([P, ENTRIES // BALL], F32, name="result")
-        early = (N_PIECES - LAST) * (PIECE // BALL)
-        nc.scalar.activation(result[:, :early], pooled[:, :early], RELU, bias=biases[2][:])
-        nc.scalar.dma_start(out[:, :early], result[:, :early])
-        nc.vector.tensor_scalar(result[:, early:], pooled[:, early:], biases[2][:], 0.0, ADD, MAX)
-        nc.sync.dma_start(out[:, early:], result[:, early:])
+        piece_balls = PIECE // BALL
+        early = slice(0, (N_PIECES - 2) * piece_balls)
+
+        def finish_on_vector(i):
+            balls = slice(i * piece_balls, (i + 1) * piece_balls)
+            nc.vector.tensor_scalar(result[:, balls], pooled[:, balls], biases[2][:], 0.0, ADD, MAX)
+
+        first_layer(range(FIRST_RUN))
+        for step in range(THIRD_EARLY + MIDDLE_LAG):
+            if step < SECOND_EARLY:
+                second_layer(step)
+            if MIDDLE_LAG <= step < MIDDLE_LAG + THIRD_EARLY:
+                third_layer(step - MIDDLE_LAG)
+        first_layer(range(FIRST_RUN, N_PIECES))
+        for step in range(SECOND_EARLY, len(CHUNKS) + LAST_LAG):
+            if step < len(CHUNKS):
+                second_layer(step)
+            if step - LAST_LAG >= THIRD_EARLY:
+                third_layer(step - LAST_LAG)
+                if chunk_entries[step - LAST_LAG].stop == (N_PIECES - 1) * PIECE:
+                    finish_on_vector(N_PIECES - 2)
+        nc.scalar.activation(result[:, early], pooled[:, early], RELU, bias=biases[2][:])
+        nc.scalar.dma_start(out[:, early], result[:, early])
+        finish_on_vector(N_PIECES - 1)
+        nc.sync.dma_start(out[:, early.stop :], result[:, early.stop :])

@@ -85,7 +85,7 @@ def tile_setabstraction_kernel(tc, table, w1, b1, w2, b2, w3, b3, offs, out):
                 else:
                     columns = columns.rearrange("d (p j) -> d p j", j=blocks)
                     in_point_order = flipped[:].rearrange("d j p -> d p j")
-                if n_units % 2 == 0:
+                if n_units % 2 == 0 and g not in BLOCKWISE:
                     nc.vector.tensor_copy(columns, in_point_order)
                 else:
                     nc.scalar.copy(columns, in_point_order)

import concourse.mybir as mybir
from concourse.masks import make_identity

BF16, F32, U16 = mybir.dt.bfloat16, mybir.dt.float32, mybir.dt.uint16
ADD, MAX = mybir.AluOpType.add, mybir.AluOpType.max
RELU = mybir.ActivationFunctionType.Relu

P = 128
POINTS = 4096
ENTRIES = 4096
BALL = 8
PIECE = 512
N_PIECES = ENTRIES // PIECE
GROUP = 4
N_GROUPS = POINTS // (GROUP * P)
UNITS = (2,) + (1,) * (N_GROUPS - 2) + (2,)
BLOCKWISE = range(N_GROUPS - 2, N_GROUPS)
WARM_UP = 3
CHUNKS = (PIECE // 2,) * (2 * N_PIECES - 1) + (PIECE // 4,) * 2
FIRST_RUN = 5
SECOND_EARLY = 2 * FIRST_RUN
THIRD_EARLY = 8
N_HALVED = 24 - SECOND_EARLY - THIRD_EARLY
MIDDLE_LAG, LAST_LAG = 6, 3
VECTOR_H2 = (*range(0, MIDDLE_LAG, 2), SECOND_EARLY)

FLOPS = 2 * ENTRIES * P * P * 3


def tile_setabstraction_kernel(tc, table, w1, b1, w2, b2, w3, b3, offs, out):
    nc = tc.nc
    with (
        tc.tile_pool(name="held", bufs=1) as held,
        tc.psum_pool(name="psum", bufs=8) as psum,
    ):
        zeros = held.tile([P, PIECE], BF16, name="zeros")
        nc.vector.memset(zeros[:], 0.0)

        def idle_matmul():
            unread = psum.tile([P, PIECE], F32, name="unread", tag="bank")
            nc.tensor.matmul(unread[:], zeros[:, :P], zeros[:], start=True, stop=True)

        for n in range(WARM_UP):
            idle_matmul()

        identity = held.tile([P, P], BF16, name="identity")
        make_identity(nc, identity[:])

        rows = held.tile([P, N_GROUPS, GROUP, P], BF16, name="rows")
        for g in range(N_GROUPS):
            group_points = table[g * GROUP * P : (g + 1) * GROUP * P, :]
            nc.sync.dma_start(
                rows[:, g, :, :].rearrange("p (u j) d -> p u j d", u=UNITS[g]),
                group_points.rearrange(
                    "(u j p) d -> p u j d" if g in BLOCKWISE else "(u p j) d -> p u j d", u=UNITS[g], p=P
                ),
            )
        offsets = held.tile([P, ENTRIES // 16], U16, name="offsets")
        nc.sync.dma_start(offsets[:], offs)
        weights = [held.tile([P, P], BF16, name=f"w{layer}") for layer in range(3)]
        biases = [held.tile([P, 1], F32, name=f"b{layer}") for layer in range(3)]
        nc.gpsimd.dma_start(weights[0][:], w1)
        nc.gpsimd.dma_start(biases[0][:], b1)
        for layer, (w, b) in enumerate(((w2, b2), (w3, b3)), start=1):
            nc.sync.dma_start(weights[layer][:], w)
            nc.sync.dma_start(biases[layer][:], b)

        scratch = held.tile([P, 1], F32, name="scratch")
        nc.vector.memset(scratch[:], 0.0)
        nc.scalar.activation(scratch[:], scratch[:], RELU)

        window = held.tile([P, POINTS], BF16, name="window")
        n_units = 0
        for g in range(N_GROUPS):
            blocks = GROUP // UNITS[g]
            for u in range(UNITS[g]):
                flipped = psum.tile([P, blocks, P], BF16, name="flipped", tag="bank")
                for j in range(blocks):
                    nc.tensor.transpose(flipped[:, j, :], rows[:, g, u * blocks + j, :], identity[:])
                first = (g * GROUP + u * blocks) * P
                columns = window[:, first : first + blocks * P]
                if g in BLOCKWISE:
                    columns = columns.rearrange("d (j p) -> d j p", j=blocks)
                    in_point_order = flipped[:]
                else:
                    columns = columns.rearrange("d (p j) -> d p j", j=blocks)
                    in_point_order = flipped[:].rearrange("d j p -> d p j")
                if n_units % 2 == 0 and g not in BLOCKWISE:
                    nc.vector.tensor_copy(columns, in_point_order)
                else:
                    nc.scalar.copy(columns, in_point_order)
                n_units += 1
            if g % 2 == 1:
                idle_matmul()

        h1 = held.tile([P, ENTRIES], BF16, name="h1")
        h2 = held.tile([P, ENTRIES], BF16, name="h2")
        pooled = held.tile([P, ENTRIES // BALL], F32, name="pooled")

        def first_layer(pieces):
            for i in pieces:
                sum1 = psum.tile([P, PIECE], F32, name="sum1", tag="bank")
                looked_up = window[:].indirect(offsets[:, i * (PIECE // 16) : (i + 1) * (PIECE // 16)])
                nc.tensor.matmul(sum1[:], weights[0][:], looked_up, start=True, stop=True)
                piece = slice(i * PIECE, (i + 1) * PIECE)
                if (i - pieces[0]) % 2 == 0:
                    nc.scalar.activation(h1[:, piece], sum1[:], RELU, bias=biases[0][:])
                else:
                    nc.vector.tensor_scalar(h1[:, piece], sum1[:], biases[0][:], 0.0, ADD, MAX)

        chunk_entries = [slice(sum(CHUNKS[:c]), sum(CHUNKS[: c + 1])) for c in range(len(CHUNKS))]

        def plain_product(layer, source, c, parts):
            total = psum.tile([P, CHUNKS[c]], F32, name="total", tag="bank")
            width = CHUNKS[c] // parts
            for n in range(parts):
                first = chunk_entries[c].start + n * width
                nc.tensor.matmul(
                    total[:, n * width : (n + 1) * width],
                    weights[layer][:],
                    source[:, first : first + width],
                    start=True,
                    stop=True,
                )
            return total

        def second_layer(c):
            sum2 = plain_product(1, h1, c, 1)
            if c in VECTOR_H2:
                nc.vector.tensor_scalar(h2[:, chunk_entries[c]], sum2[:], biases[1][:], 0.0, ADD, MAX)
            else:
                nc.scalar.activation(h2[:, chunk_entries[c]], sum2[:], RELU, bias=biases[1][:])

        def third_layer(c):
            sum3 = plain_product(2, h2, c, 2 if c < N_HALVED else 1)
            balls = slice(chunk_entries[c].start // BALL, chunk_entries[c].stop // BALL)
            nc.vector.tensor_reduce(
                pooled[:, balls], sum3[:].rearrange("r (q k) -> r q k", k=BALL), mybir.AxisListType.X, MAX
            )

        result = held.tile([P, ENTRIES // BALL], F32, name="result")
        piece_balls = PIECE // BALL
        early = slice(0, (N_PIECES - 2) * piece_balls)

        def finish_on_vector(i):
            balls = slice(i * piece_balls, (i + 1) * piece_balls)
            nc.vector.tensor_scalar(result[:, balls], pooled[:, balls], biases[2][:], 0.0, ADD, MAX)

        first_layer(range(FIRST_RUN))
        for step in range(THIRD_EARLY + MIDDLE_LAG):
            if step < SECOND_EARLY:
                second_layer(step)
            if MIDDLE_LAG <= step < MIDDLE_LAG + THIRD_EARLY:
                third_layer(step - MIDDLE_LAG)
        first_layer(range(FIRST_RUN, N_PIECES))
        for step in range(SECOND_EARLY, len(CHUNKS) + LAST_LAG):
            if step < len(CHUNKS):
                second_layer(step)
            if step - LAST_LAG >= THIRD_EARLY:
                third_layer(step - LAST_LAG)
                if chunk_entries[step - LAST_LAG].stop == (N_PIECES - 1) * PIECE:
                    finish_on_vector(N_PIECES - 2)
        nc.scalar.activation(result[:, early], pooled[:, early], RELU, bias=biases[2][:])
        nc.scalar.dma_start(out[:, early], result[:, early])
        finish_on_vector(N_PIECES - 1)
        nc.sync.dma_start(out[:, early.stop :], result[:, early.stop :])
